import numpy as np
import ml_dtypes


def mxq(x, axis, fmt="e4m3"):
    dtype, down = {"e4m3": (ml_dtypes.float8_e4m3fn, 7), "e5m2": (ml_dtypes.float8_e5m2, 14)}[fmt]
    v = np.moveaxis(np.asarray(x, np.float32).astype(ml_dtypes.bfloat16).astype(np.float64), axis, -1)
    blocks = v.reshape(v.shape[:-1] + (-1, 32))
    amax = np.abs(blocks).max(-1, keepdims=True)
    byte = np.maximum(np.where(amax > 0, np.frexp(amax)[1] - 1 + 127, 0) - down, 1)
    scale = np.exp2(byte - 127.0)
    codes = (blocks / scale).astype(np.float32).astype(dtype).astype(np.float64)
    return np.moveaxis((codes * scale).reshape(v.shape), -1, axis)


WIDE = False


def mx_kscale(k):
    if not WIDE:
        return np.ones(k)
    levels = np.array([10, -10, 5, -5, 0])
    a = np.random.permutation(np.resize(levels, k // 512 * 4)).reshape(k // 512, 4)
    idx = np.arange(k)
    return np.exp2(a[idx // 512, idx % 128 // 32])


BF16 = ml_dtypes.bfloat16


def bf(x):
    return np.asarray(x, np.float32).astype(BF16)


def f64(x):
    return np.asarray(x).astype(np.float64)


E2M1 = np.array([0.0, 0.5, 1.0, 1.5, 2.0, 3.0, 4.0, 6.0, -0.0, -0.5, -1.0, -1.5, -2.0, -3.0, -4.0, -6.0])


def pack_weight(w, fmt):
    k, n = w.shape
    w = f64(bf(w)).reshape(k // 32, 32, n)
    amax = np.abs(w).max(1)
    if fmt == "e4m3":
        byte = np.frexp(amax)[1] - 1 + 127 - 7
    else:
        mant, ex = np.frexp(amax / 6.0)
        byte = np.where(mant > 0.5, ex, ex - 1) + 127
    byte = np.clip(np.where(amax > 0, byte, 1), 1, 254)
    scaled = (w * np.exp2(127.0 - byte)[:, None, :]).reshape(k, n).astype(np.float32)
    by_word = np.ascontiguousarray(scaled.reshape(k // 512, 128, 4, n).transpose(0, 1, 3, 2))
    if fmt == "e4m3":
        words = by_word.astype(ml_dtypes.float8_e4m3fn).view(np.uint8)
    else:
        c = by_word.astype(ml_dtypes.float4_e2m1fn).view(np.uint8) & 0xF
        words = c[..., 0::2] | (c[..., 1::2] << 4)
    return np.ascontiguousarray(words), np.ascontiguousarray(byte.astype(np.uint8).reshape(k // 512, 16, n))


def unpack_weight(words, scales, fmt):
    g, p, n, _ = words.shape
    if fmt == "e4m3":
        vals = np.ascontiguousarray(words).view(ml_dtypes.float8_e4m3fn).astype(np.float64)
    else:
        nib = np.empty((g, p, n, 4), np.uint8)
        nib[..., 0::2] = words & 0xF
        nib[..., 1::2] = words >> 4
        vals = E2M1[nib]
    vals = vals * np.repeat(np.exp2(scales.astype(np.float64) - 127.0), 8, axis=1)[..., None]
    return vals.transpose(0, 1, 3, 2).reshape(g * 512, n)

def pack4(w):
    words, scales = pack_weight(w, "e2m1")
    return words.reshape(words.shape[0], 128, -1), scales


def unpack4(words, scales):
    return unpack_weight(words.reshape(words.shape[0], 128, -1, 2), scales, "e2m1")


B, S, K, N = 4, 256, 4096, 1024

GRID_VALUES = np.array([-6.0, -4.0, -3.0, -2.0, -1.5, -1.0, -0.5, 0.0, 0.5, 1.0, 1.5, 2.0, 3.0, 4.0, 6.0], dtype=np.float32)


def setup_inputs():
    s = mx_kscale(K)
    x = bf(np.random.standard_normal((B, S, K)) * s)
    weight = np.random.standard_normal((N, K)) * 0.02 / s[None, :]
    weight_words, weight_scales = pack4(np.ascontiguousarray(weight.T))
    bias = bf(np.random.standard_normal(N) * 0.3)
    return {"x": x,
            "weight_words": weight_words,
            "weight_scales": weight_scales,
            "bias": bias,
            "grid": bf(GRID_VALUES)}


def reference(x, weight_words, weight_scales, bias, grid):
    x, bias, grid = f64(x), f64(bias), f64(grid)
    wt = unpack4(weight_words, weight_scales)
    out_shape = x.shape[:-1] + (wt.shape[1],)
    x2d = x.reshape(-1, x.shape[-1])
    out = (mxq(x2d, 1, "e4m3") @ wt) + bias
    return out.reshape(out_shape)

@@ -1,0 +1,246 @@
+from contextlib import ExitStack
+
+import concourse.mybir as mybir
+from concourse.masks import make_identity
+
+BF16 = mybir.dt.bfloat16
+F32 = mybir.dt.float32
+I32 = mybir.dt.int32
+U8 = mybir.dt.uint8
+U32 = mybir.dt.uint32
+FP8X4 = mybir.dt.float8_e4m3fn_x4
+FP4X4 = mybir.dt.float4_e2m1fn_x4
+
+P = 128
+M, K, N = 1024, 4096, 1024
+FLOPS = 2 * M * K * N
+
+NH = 512
+QT = 4
+CG = 2
+NCH = 4
+
+GROUPS = [
+    [[0], [1], [2], [3]],
+    [[0], [1], [2], [3]],
+    [[0, 1], [2, 3]],
+    [[0, 1], [2, 3]],
+    [[0, 1], [2, 3]],
+    [[0, 1], [2, 3]],
+    [[0, 1], [2, 3]],
+    [[0, 1], [2, 3]],
+]
+
+
+def tile_ant_linear_kernel(tc, x, weight_words, weight_scales, bias, grid, out):
+    nc = tc.nc
+    x2d = x.flatten_outer_dims()
+    out2d = out.flatten_outer_dims()
+    ww = weight_words.bitcast(I32)
+    ws = weight_scales.bitcast(I32)
+
+    with ExitStack() as ctx:
+        keep = ctx.enter_context(tc.tile_pool(name="keep", bufs=1))
+        rot = ctx.enter_context(tc.tile_pool(name="rot", bufs=4))
+        outp = ctx.enter_context(tc.tile_pool(name="outp", bufs=6))
+        tpp = ctx.enter_context(tc.psum_pool(name="tpp", bufs=4))
+        accp = ctx.enter_context(tc.psum_pool(name="accp", bufs=1))
+        ctx.enter_context(tc.manual_schedule())
+
+        plane_sets = [(0, 0, 2), (0, 2, 6), (1, 0, 8)]
+        planes = []
+        pmap = {}
+        for i, (h, g0, ng) in enumerate(plane_sets):
+            wp = keep.tile([P, ng, NH], U8, name="wp%d" % i, align_bytes=64)
+            planes.append(wp)
+            for j in range(ng):
+                pmap[(h, g0 + j)] = (wp, j)
+        bias_row = keep.tile([P, N], BF16, name="bias_row")
+        bias_sb = keep.tile([P, N], F32, name="bias_sb")
+        ones = keep.tile([P, P], BF16, name="ones")
+        ident = keep.tile([P, P], F32, name="ident")
+
+        nc.vector.memset(planes[0][:].bitcast(I32), 0)
+        nc.vector.memset(bias_row[:].bitcast(I32), 0)
+        nc.vector.memset(planes[1][:].bitcast(I32), 0)
+        nc.vector.memset(planes[2][:].bitcast(I32), 0)
+        make_identity(nc, ident[:])
+        nc.gpsimd.memset(ones[:], 1.0)
+        nc.scalar.dma_start(out=bias_row[0:1, :], in_=bias.rearrange("(o n) -> o n", o=1))
+
+        xt = {}
+
+        def load_x(k):
+            q, c = divmod(k, NCH)
+            for gi, grp in enumerate(GROUPS[k]):
+                n = len(grp)
+                t = keep.tile([P, n, CG * 512], BF16, name="x%d_%d" % (k, gi))
+                r0 = (q * QT + grp[0]) * P
+                nc.sync.dma_start(
+                    out=t[:],
+                    in_=x2d[r0 : r0 + n * P, c * CG * 512 : (c + 1) * CG * 512].rearrange(
+                        "(t p) k -> p t k", p=P
+                    ),
+                )
+                xt[(k, gi)] = t
+
+        def load_planes(i):
+            h, g0, ng = plane_sets[i]
+            wpi = planes[i][:].bitcast(I32)
+            for r in range(4):
+                nc.sync.dma_start(
+                    out=wpi[r:P:32, :, :],
+                    in_=ws[g0 : g0 + ng, r:16:4, h * 128 : (h + 1) * 128].rearrange("g q n -> q g n"),
+                )
+
+        wmap = {}
+
+        def load_w(h, g0, ng):
+            t = keep.tile([P, ng, 2 * NH], U8, name="w%d_%d" % (h, g0), align_bytes=64)
+            nc.sync.dma_start(
+                out=t[:].bitcast(I32),
+                in_=ww[g0 : g0 + ng, :, h * 256 : (h + 1) * 256].rearrange("g p b -> p g b"),
+            )
+            for j in range(ng):
+                wmap[(h, g0 + j)] = (t, j)
+
+        load_x(0)
+        load_planes(0)
+        load_w(0, 0, 2)
+        load_x(1)
+        load_x(2)
+        load_planes(1)
+        load_w(0, 2, 2)
+        load_x(3)
+        load_w(0, 4, 2)
+        load_w(0, 6, 2)
+        load_planes(2)
+        load_w(1, 0, 4)
+        load_w(1, 4, 4)
+        for k in range(4, 8):
+            load_x(k)
+
+        xs = {}
+        gr = {}
+        cmap = {}
+
+        def sort(k):
+            for gi, grp in enumerate(GROUPS[k]):
+                n = len(grp)
+                s = rot.tile([P, n, CG, 2, P], F32, name="xs%d_%d" % (k, gi), tag="xs%d" % n)
+                nc.vector.tensor_copy(
+                    out=s[:],
+                    in_=xt[(k, gi)][:].bitcast(F32).rearrange("p n (g q u) -> p n g u q", g=CG, u=2),
+                )
+                xs[(k, gi)] = s
+
+        def transposes(k):
+            for gi, grp in enumerate(GROUPS[k]):
+                n = len(grp)
+                g_t = rot.tile([P, n, CG, P, 4], BF16, name="gr%d_%d" % (k, gi), tag="gr%d" % n, align_bytes=64)
+                gr[(k, gi)] = g_t
+                for j in range(n):
+                    tp = tpp.tile([P, CG, 2, P], F32, name="tp%d_%d_%d" % (k, gi, j), tag="tp")
+                    for g2 in range(CG):
+                        for u in range(2):
+                            nc.tensor.transpose(tp[:, g2, u, :], xs[(k, gi)][:, j, g2, u, :], ident[:])
+                    nc.scalar.copy(out=g_t[:, j].bitcast(F32), in_=tp[:].rearrange("p g u m -> p g m u"))
+
+        def quant(k):
+            q, c = divmod(k, NCH)
+            for gi, grp in enumerate(GROUPS[k]):
+                n = len(grp)
+                cd = keep.tile([P, n * CG * P], U32, name="cd%d_%d" % (k, gi), align_bytes=64)
+                sc = keep.tile([P, n * CG * P], U8, name="sc%d_%d" % (k, gi), align_bytes=64)
+                nc.vector.quantize_mx(
+                    out=cd[:].bitcast(FP8X4),
+                    scales=sc[:],
+                    in_=gr[(k, gi)][:].rearrange("p n g m k -> p (n g m k)"),
+                )
+                for j, t in enumerate(grp):
+                    for g2 in range(CG):
+                        cmap[(q, t, c * CG + g2)] = (cd, sc, j * CG + g2)
+
+        acc = {}
+
+        def mx(q, t, g, h):
+            cd, sc, i = cmap[(q, t, g)]
+            w, wj = wmap[(h, g)]
+            wp, pj = pmap[(h, g)]
+            if g == 0:
+                acc[t] = accp.tile([P, NH], F32, name="acc%d_%d_%d" % (q, h, t), tag="acc%d" % t)
+            nc.tensor.matmul_mx(
+                out=acc[t][:],
+                lhsT=cd[:, i * P : (i + 1) * P].bitcast(FP8X4),
+                lhsT_scale=sc[:, i * P : (i + 1) * P],
+                rhs=w[:, wj, :].bitcast(FP4X4),
+                rhs_scale=wp[:, pj, :],
+                start=(g == 0),
+                stop=(g == 7),
+            )
+
+        def finish(q, t, h):
+            o = outp.tile([P, NH], F32, name="o%d_%d_%d" % (q, h, t), tag="o")
+            nc.vector.tensor_tensor(
+                out=o[:], in0=acc[t][:], in1=bias_sb[:, h * NH : (h + 1) * NH], op=mybir.AluOpType.add
+            )
+            r0 = (q * QT + t) * P
+            nc.sync.dma_start(out=out2d[r0 : r0 + P, h * NH : (h + 1) * NH], in_=o[:])
+
+        def run_chunk(q, c):
+            for t in range(QT):
+                for g2 in range(CG):
+                    mx(q, t, c * CG + g2, 0)
+                if c == NCH - 1:
+                    finish(q, t, 0)
+
+        def run_tile(q, t):
+            for g in range(8):
+                mx(q, t, g, 1)
+            finish(q, t, 1)
+
+        def bias_spread():
+            for h in range(2):
+                bp = tpp.tile([P, NH], F32, name="bp%d" % h, tag="tp")
+                nc.tensor.matmul(bp[:], lhsT=ones[:], rhs=bias_row[:, h * NH : (h + 1) * NH], start=True, stop=True)
+                nc.scalar.copy(out=bias_sb[:, h * NH : (h + 1) * NH], in_=bp[:])
+
+        sort(0)
+        transposes(0)
+        quant(0)
+        run_chunk(0, 0)
+        sort(1)
+        transposes(1)
+        sort(2)
+        quant(1)
+        transposes(2)
+        run_chunk(0, 1)
+        sort(3)
+        quant(2)
+        transposes(3)
+        run_chunk(0, 2)
+        quant(3)
+        bias_spread()
+        run_chunk(0, 3)
+        sort(4)
+        run_tile(0, 0)
+        run_tile(0, 1)
+        transposes(4)
+        sort(5)
+        quant(4)
+        run_tile(0, 2)
+        transposes(5)
+        sort(6)
+        quant(5)
+        run_tile(0, 3)
+        transposes(6)
+        sort(7)
+        quant(6)
+        run_chunk(1, 0)
+        transposes(7)
+        quant(7)
+        run_chunk(1, 1)
+        run_chunk(1, 2)
+        run_chunk(1, 3)
+        for t in range(QT):
+            run_tile(1, t)

@@ -187,8 +187,8 @@ def tile_ant_linear_kernel(tc, x, weight_words, weight_scales, bias, grid, out):
             r0 = (q * QT + t) * P
             nc.sync.dma_start(out=out2d[r0 : r0 + P, h * NH : (h + 1) * NH], in_=o[:])
 
-        def run_chunk(q, c):
-            for t in range(QT):
+        def run_chunk(q, c, tiles=(0, 1, 2, 3)):
+            for t in tiles:
                 for g2 in range(CG):
                     mx(q, t, c * CG + g2, 0)
                 if c == NCH - 1:
@@ -208,9 +208,10 @@ def tile_ant_linear_kernel(tc, x, weight_words, weight_scales, bias, grid, out):
         sort(0)
         transposes(0)
         quant(0)
-        run_chunk(0, 0)
+        run_chunk(0, 0, (0, 1))
         sort(1)
         transposes(1)
+        run_chunk(0, 0, (2, 3))
         sort(2)
         quant(1)
         transposes(2)

@@ -23,8 +23,8 @@ NCH = 4
 GROUPS = [
     [[0], [1], [2], [3]],
     [[0], [1], [2], [3]],
-    [[0, 1], [2, 3]],
-    [[0, 1], [2, 3]],
+    [[0], [1], [2], [3]],
+    [[0], [1], [2], [3]],
     [[0, 1], [2, 3]],
     [[0, 1], [2, 3]],
     [[0, 1], [2, 3]],
@@ -59,13 +59,15 @@ def tile_ant_linear_kernel(tc, x, weight_words, weight_scales, bias, grid, out):
         bias_sb = keep.tile([P, N], F32, name="bias_sb")
         ones = keep.tile([P, P], BF16, name="ones")
         ident = keep.tile([P, P], F32, name="ident")
+        zeros = keep.tile([P, NH], BF16, name="zeros")
 
-        nc.vector.memset(planes[0][:].bitcast(I32), 0)
+        nc.gpsimd.memset(ones[:], 1.0)
         nc.vector.memset(bias_row[:].bitcast(I32), 0)
+        nc.vector.memset(zeros[:].bitcast(I32), 0)
+        nc.vector.memset(planes[0][:].bitcast(I32), 0)
         nc.vector.memset(planes[1][:].bitcast(I32), 0)
         nc.vector.memset(planes[2][:].bitcast(I32), 0)
         make_identity(nc, ident[:])
-        nc.gpsimd.memset(ones[:], 1.0)
         nc.scalar.dma_start(out=bias_row[0:1, :], in_=bias.rearrange("(o n) -> o n", o=1))
 
         xt = {}
@@ -105,14 +107,14 @@ def tile_ant_linear_kernel(tc, x, weight_words, weight_scales, bias, grid, out):
                 wmap[(h, g0 + j)] = (t, j)
 
         load_x(0)
-        load_planes(0)
         load_w(0, 0, 2)
+        load_planes(0)
         load_x(1)
-        load_x(2)
-        load_planes(1)
         load_w(0, 2, 2)
-        load_x(3)
+        load_planes(1)
+        load_x(2)
         load_w(0, 4, 2)
+        load_x(3)
         load_w(0, 6, 2)
         load_planes(2)
         load_w(1, 0, 4)
@@ -134,7 +136,13 @@ def tile_ant_linear_kernel(tc, x, weight_words, weight_scales, bias, grid, out):
                 )
                 xs[(k, gi)] = s
 
-        def transposes(k):
+        junk = accp.tile([P, NH], F32, name="junk", tag="acc0")
+
+        def dummies(n):
+            for i in range(n):
+                nc.tensor.matmul(junk[:], lhsT=ones[:], rhs=zeros[:], start=True, stop=True)
+
+        def transposes(k, fill=()):
             for gi, grp in enumerate(GROUPS[k]):
                 n = len(grp)
                 g_t = rot.tile([P, n, CG, P, 4], BF16, name="gr%d_%d" % (k, gi), tag="gr%d" % n, align_bytes=64)
@@ -145,6 +153,8 @@ def tile_ant_linear_kernel(tc, x, weight_words, weight_scales, bias, grid, out):
                         for u in range(2):
                             nc.tensor.transpose(tp[:, g2, u, :], xs[(k, gi)][:, j, g2, u, :], ident[:])
                     nc.scalar.copy(out=g_t[:, j].bitcast(F32), in_=tp[:].rearrange("p g u m -> p g m u"))
+                    if grp[j] in fill:
+                        dummies(1)
 
         def quant(k):
             q, c = divmod(k, NCH)
@@ -201,28 +211,24 @@ def tile_ant_linear_kernel(tc, x, weight_words, weight_scales, bias, grid, out):
 
         def bias_spread():
             for h in range(2):
-                bp = tpp.tile([P, NH], F32, name="bp%d" % h, tag="tp")
+                bp = accp.tile([P, NH], F32, name="bp%d" % h, tag="acc%d" % (2 + h))
                 nc.tensor.matmul(bp[:], lhsT=ones[:], rhs=bias_row[:, h * NH : (h + 1) * NH], start=True, stop=True)
                 nc.scalar.copy(out=bias_sb[:, h * NH : (h + 1) * NH], in_=bp[:])
 
+        lo, hi = (0, 1), (2, 3)
+        dummies(6)
         sort(0)
-        transposes(0)
-        quant(0)
-        run_chunk(0, 0, (0, 1))
-        sort(1)
-        transposes(1)
-        run_chunk(0, 0, (2, 3))
-        sort(2)
-        quant(1)
-        transposes(2)
-        run_chunk(0, 1)
-        sort(3)
-        quant(2)
-        transposes(3)
-        run_chunk(0, 2)
-        quant(3)
+        transposes(0, fill=(1, 3))
         bias_spread()
-        run_chunk(0, 3)
+        quant(0)
+        run_chunk(0, 0, lo)
+        for c in (1, 2, 3):
+            sort(c)
+            transposes(c)
+            run_chunk(0, c - 1, hi)
+            quant(c)
+            run_chunk(0, c, lo)
+        run_chunk(0, 3, hi)
         sort(4)
         run_tile(0, 0)
         run_tile(0, 1)

@@ -14,22 +14,31 @@ FP4X4 = mybir.dt.float4_e2m1fn_x4
 P = 128
 M, K, N = 1024, 4096, 1024
 FLOPS = 2 * M * K * N
-
 NH = 512
-QT = 4
-CG = 2
-NCH = 4
+NG = 8
 
-GROUPS = [
-    [[0], [1], [2], [3]],
-    [[0], [1], [2], [3]],
-    [[0], [1], [2], [3]],
-    [[0], [1], [2], [3]],
-    [[0, 1], [2, 3]],
-    [[0, 1], [2, 3]],
-    [[0, 1], [2, 3]],
-    [[0, 1], [2, 3]],
-]
+GROUPS = {
+    "c0t0": ((0,), 0, 2),
+    "c0t1": ((1,), 0, 2),
+    "c0t2": ((2,), 0, 2),
+    "c0t3": ((3,), 0, 2),
+    "c1t0": ((0,), 2, 2),
+    "c1t1": ((1,), 2, 2),
+    "c1t2": ((2,), 2, 2),
+    "c1t3": ((3,), 2, 2),
+    "c2t0": ((0, 1), 4, 2),
+    "c2t2": ((2, 3), 4, 2),
+    "c3t0": ((0, 1), 6, 2),
+    "c3t2": ((2, 3), 6, 2),
+    "T4": ((4,), 0, 8),
+    "T5": ((5,), 0, 8),
+}
+CHUNK = {
+    0: ["c0t0", "c0t1", "c0t2", "c0t3"],
+    1: ["c1t0", "c1t1", "c1t2", "c1t3"],
+    2: ["c2t0", "c2t2"],
+    3: ["c3t0", "c3t2"],
+}
 
 
 def tile_ant_linear_kernel(tc, x, weight_words, weight_scales, bias, grid, out):
@@ -41,8 +50,8 @@ def tile_ant_linear_kernel(tc, x, weight_words, weight_scales, bias, grid, out):
 
     with ExitStack() as ctx:
         keep = ctx.enter_context(tc.tile_pool(name="keep", bufs=1))
-        rot = ctx.enter_context(tc.tile_pool(name="rot", bufs=4))
-        outp = ctx.enter_context(tc.tile_pool(name="outp", bufs=6))
+        rot = ctx.enter_context(tc.tile_pool(name="rot", bufs=2))
+        outp = ctx.enter_context(tc.tile_pool(name="outp", bufs=4))
         tpp = ctx.enter_context(tc.psum_pool(name="tpp", bufs=4))
         accp = ctx.enter_context(tc.psum_pool(name="accp", bufs=1))
         ctx.enter_context(tc.manual_schedule())
@@ -59,32 +68,31 @@ def tile_ant_linear_kernel(tc, x, weight_words, weight_scales, bias, grid, out):
         bias_sb = keep.tile([P, N], F32, name="bias_sb")
         ones = keep.tile([P, P], BF16, name="ones")
         ident = keep.tile([P, P], F32, name="ident")
-        zeros = keep.tile([P, NH], BF16, name="zeros")
 
-        nc.gpsimd.memset(ones[:], 1.0)
-        nc.vector.memset(bias_row[:].bitcast(I32), 0)
-        nc.vector.memset(zeros[:].bitcast(I32), 0)
         nc.vector.memset(planes[0][:].bitcast(I32), 0)
+        nc.vector.memset(bias_row[:].bitcast(I32), 0)
         nc.vector.memset(planes[1][:].bitcast(I32), 0)
         nc.vector.memset(planes[2][:].bitcast(I32), 0)
         make_identity(nc, ident[:])
+        nc.gpsimd.memset(ones[:], 1.0)
         nc.scalar.dma_start(out=bias_row[0:1, :], in_=bias.rearrange("(o n) -> o n", o=1))
 
         xt = {}
 
-        def load_x(k):
-            q, c = divmod(k, NCH)
-            for gi, grp in enumerate(GROUPS[k]):
-                n = len(grp)
-                t = keep.tile([P, n, CG * 512], BF16, name="x%d_%d" % (k, gi))
-                r0 = (q * QT + grp[0]) * P
-                nc.sync.dma_start(
-                    out=t[:],
-                    in_=x2d[r0 : r0 + n * P, c * CG * 512 : (c + 1) * CG * 512].rearrange(
-                        "(t p) k -> p t k", p=P
-                    ),
-                )
-                xt[(k, gi)] = t
+        def load_x(name):
+            tiles, g0, ng = GROUPS[name]
+            n = len(tiles)
+            t = keep.tile([P, n, ng * 512], BF16, name="x_" + name)
+            r0 = tiles[0] * P
+            nc.sync.dma_start(
+                out=t[:],
+                in_=x2d[r0 : r0 + n * P, g0 * 512 : (g0 + ng) * 512].rearrange("(t p) k -> p t k", p=P),
+            )
+            xt[name] = t
+
+        def load_chunk(c):
+            for name in CHUNK[c]:
+                load_x(name)
 
         def load_planes(i):
             h, g0, ng = plane_sets[i]
@@ -106,148 +114,211 @@ def tile_ant_linear_kernel(tc, x, weight_words, weight_scales, bias, grid, out):
             for j in range(ng):
                 wmap[(h, g0 + j)] = (t, j)
 
-        load_x(0)
-        load_w(0, 0, 2)
+        xv = {}
+
+        def load_v(t):
+            v = keep.tile([P, 4 * NG, P], BF16, name="xv%d" % t)
+            src = x2d[t * P : (t + 1) * P, :].rearrange("(j mb) (g kb kk) -> kb j mb g kk", mb=4, kb=4, kk=P)
+            for kb in range(4):
+                nc.sync.dma_start(
+                    out=v[32 * kb : 32 * kb + 32].rearrange("p (mb g) kk -> p mb g kk", mb=4), in_=src[kb]
+                )
+            xv[t] = v
+
+        load_chunk(0)
         load_planes(0)
-        load_x(1)
-        load_w(0, 2, 2)
+        load_w(0, 0, 2)
+        load_chunk(1)
+        load_chunk(2)
         load_planes(1)
-        load_x(2)
+        load_w(0, 2, 2)
+        load_chunk(3)
         load_w(0, 4, 2)
-        load_x(3)
         load_w(0, 6, 2)
         load_planes(2)
         load_w(1, 0, 4)
         load_w(1, 4, 4)
-        for k in range(4, 8):
-            load_x(k)
+        load_x("T4")
+        load_x("T5")
+        load_v(6)
+        load_v(7)
 
         xs = {}
         gr = {}
         cmap = {}
 
-        def sort(k):
-            for gi, grp in enumerate(GROUPS[k]):
-                n = len(grp)
-                s = rot.tile([P, n, CG, 2, P], F32, name="xs%d_%d" % (k, gi), tag="xs%d" % n)
-                nc.vector.tensor_copy(
-                    out=s[:],
-                    in_=xt[(k, gi)][:].bitcast(F32).rearrange("p n (g q u) -> p n g u q", g=CG, u=2),
-                )
-                xs[(k, gi)] = s
+        def sort(name):
+            tiles, g0, ng = GROUPS[name]
+            n = len(tiles)
+            s = rot.tile([P, n, ng, 2, P], F32, name="xs_" + name, tag="xs%d" % (n * ng), bufs=4 if n * ng == 2 else 2)
+            nc.vector.tensor_copy(
+                out=s[:], in_=xt[name][:].bitcast(F32).rearrange("p n (g q u) -> p n g u q", g=ng, u=2)
+            )
+            xs[name] = s
 
-        junk = accp.tile([P, NH], F32, name="junk", tag="acc0")
-
-        def dummies(n):
-            for i in range(n):
-                nc.tensor.matmul(junk[:], lhsT=ones[:], rhs=zeros[:], start=True, stop=True)
-
-        def transposes(k, fill=()):
-            for gi, grp in enumerate(GROUPS[k]):
-                n = len(grp)
-                g_t = rot.tile([P, n, CG, P, 4], BF16, name="gr%d_%d" % (k, gi), tag="gr%d" % n, align_bytes=64)
-                gr[(k, gi)] = g_t
-                for j in range(n):
-                    tp = tpp.tile([P, CG, 2, P], F32, name="tp%d_%d_%d" % (k, gi, j), tag="tp")
-                    for g2 in range(CG):
+        def transposes(name):
+            tiles, g0, ng = GROUPS[name]
+            n = len(tiles)
+            g_t = rot.tile(
+                [P, n, ng, P, 4], BF16, name="gr_" + name, tag="gr%d" % (n * ng), bufs=4 if n * ng == 2 else 2,
+                align_bytes=64,
+            )
+            gr[name] = g_t
+            for j in range(n):
+                for gp in range(ng // 2):
+                    tp = tpp.tile([P, 2, 2, P], F32, name="tp_%s_%d_%d" % (name, j, gp), tag="tp")
+                    for g2 in range(2):
                         for u in range(2):
-                            nc.tensor.transpose(tp[:, g2, u, :], xs[(k, gi)][:, j, g2, u, :], ident[:])
-                    nc.scalar.copy(out=g_t[:, j].bitcast(F32), in_=tp[:].rearrange("p g u m -> p g m u"))
-                    if grp[j] in fill:
-                        dummies(1)
+                            nc.tensor.transpose(tp[:, g2, u, :], xs[name][:, j, 2 * gp + g2, u, :], ident[:])
+                    nc.scalar.copy(
+                        out=g_t[:, j, 2 * gp : 2 * gp + 2].bitcast(F32), in_=tp[:].rearrange("p g u m -> p g m u")
+                    )
 
-        def quant(k):
-            q, c = divmod(k, NCH)
-            for gi, grp in enumerate(GROUPS[k]):
-                n = len(grp)
-                cd = keep.tile([P, n * CG * P], U32, name="cd%d_%d" % (k, gi), align_bytes=64)
-                sc = keep.tile([P, n * CG * P], U8, name="sc%d_%d" % (k, gi), align_bytes=64)
-                nc.vector.quantize_mx(
-                    out=cd[:].bitcast(FP8X4),
-                    scales=sc[:],
-                    in_=gr[(k, gi)][:].rearrange("p n g m k -> p (n g m k)"),
+        def quantise(name, tiles, g0, ng, grouped):
+            n = len(tiles)
+            cd = keep.tile([P, n * ng * P], U32, name="cd_" + name, align_bytes=64)
+            sc = keep.tile([P, n * ng * P], U8, name="sc_" + name, align_bytes=64)
+            nc.vector.quantize_mx(out=cd[:].bitcast(FP8X4), scales=sc[:], in_=grouped)
+            for j, t in enumerate(tiles):
+                for g in range(ng):
+                    cmap[(t, g0 + g)] = (cd, sc, j * ng + g)
+
+        def quant(name):
+            tiles, g0, ng = GROUPS[name]
+            quantise(name, tiles, g0, ng, gr[name][:].rearrange("p n g m k -> p (n g m k)"))
+
+        s1 = {}
+        o1 = {}
+        grv = {}
+
+        def v_sort(t, a):
+            s = rot.tile([P, 2 * NG, 2, 32], F32, name="s1_%d_%d" % (t, a), tag="s1", align_bytes=64)
+            nc.scalar.copy(
+                out=s[:],
+                in_=xv[t][:, 2 * NG * a : 2 * NG * (a + 1)].bitcast(F32).rearrange("p b (i u) -> p b u i", u=2),
+            )
+            s1[(t, a)] = s
+
+        def v_transpose(t, a):
+            o = rot.tile([P, 2 * NG, 2, 32], F32, name="o1_%d_%d" % (t, a), tag="o1", align_bytes=64)
+            nc.vector.transpose(
+                out=o[:].rearrange("p b u j -> p (b u j)"), in_=s1[(t, a)][:].rearrange("p b u i -> p (b u i)")
+            )
+            o1[(t, a)] = o
+
+        def v_group(t):
+            g_t = rot.tile([P, 1, NG, P, 4], BF16, name="grv%d" % t, tag="gr8", align_bytes=64)
+            grv[t] = g_t
+            gf = g_t[:, 0].bitcast(F32)
+            for mb in range(4):
+                a, m2 = divmod(mb, 2)
+                nc.scalar.copy(
+                    out=gf[:, :, 32 * mb : 32 * mb + 32, :],
+                    in_=o1[(t, a)][:, NG * m2 : NG * (m2 + 1)].rearrange("p g u j -> p g j u"),
                 )
-                for j, t in enumerate(grp):
-                    for g2 in range(CG):
-                        cmap[(q, t, c * CG + g2)] = (cd, sc, j * CG + g2)
+
+        def v_quant(t):
+            quantise("v%d" % t, (t,), 0, NG, grv[t][:].rearrange("p n g m k -> p (n g m k)"))
 
         acc = {}
 
-        def mx(q, t, g, h):
-            cd, sc, i = cmap[(q, t, g)]
+        def mx(t, g, h, bank):
+            cd, sc, i = cmap[(t, g)]
             w, wj = wmap[(h, g)]
             wp, pj = pmap[(h, g)]
             if g == 0:
-                acc[t] = accp.tile([P, NH], F32, name="acc%d_%d_%d" % (q, h, t), tag="acc%d" % t)
+                acc[bank] = accp.tile([P, NH], F32, name="acc%d_%d" % (t, h), tag="acc%d" % bank)
             nc.tensor.matmul_mx(
-                out=acc[t][:],
+                out=acc[bank][:],
                 lhsT=cd[:, i * P : (i + 1) * P].bitcast(FP8X4),
                 lhsT_scale=sc[:, i * P : (i + 1) * P],
                 rhs=w[:, wj, :].bitcast(FP4X4),
                 rhs_scale=wp[:, pj, :],
                 start=(g == 0),
-                stop=(g == 7),
+                stop=(g == NG - 1),
             )
 
-        def finish(q, t, h):
-            o = outp.tile([P, NH], F32, name="o%d_%d_%d" % (q, h, t), tag="o")
+        def finish(t, h, bank):
+            o = outp.tile([P, NH], F32, name="o%d_%d" % (t, h), tag="o")
             nc.vector.tensor_tensor(
-                out=o[:], in0=acc[t][:], in1=bias_sb[:, h * NH : (h + 1) * NH], op=mybir.AluOpType.add
+                out=o[:], in0=acc[bank][:], in1=bias_sb[:, h * NH : (h + 1) * NH], op=mybir.AluOpType.add
             )
-            r0 = (q * QT + t) * P
-            nc.sync.dma_start(out=out2d[r0 : r0 + P, h * NH : (h + 1) * NH], in_=o[:])
+            r0 = t * P
+            if t in xv:
+                for mb in range(4):
+                    nc.sync.dma_start(
+                        out=out2d[r0 + mb : r0 + P : 4, h * NH : (h + 1) * NH], in_=o[32 * mb : 32 * mb + 32, :]
+                    )
+            else:
+                nc.sync.dma_start(out=out2d[r0 : r0 + P, h * NH : (h + 1) * NH], in_=o[:])
 
-        def run_chunk(q, c, tiles=(0, 1, 2, 3)):
+        def run_chunk(c, tiles=(0, 1, 2, 3)):
             for t in tiles:
-                for g2 in range(CG):
-                    mx(q, t, c * CG + g2, 0)
-                if c == NCH - 1:
-                    finish(q, t, 0)
+                for g2 in range(2):
+                    mx(t, 2 * c + g2, 0, t)
+                if c == 3:
+                    finish(t, 0, t)
 
-        def run_tile(q, t):
-            for g in range(8):
-                mx(q, t, g, 1)
-            finish(q, t, 1)
+        def run_bank(t, h, bank):
+            for g in range(NG):
+                mx(t, g, h, bank)
+            finish(t, h, bank)
 
         def bias_spread():
             for h in range(2):
-                bp = accp.tile([P, NH], F32, name="bp%d" % h, tag="acc%d" % (2 + h))
+                bp = tpp.tile([P, NH], F32, name="bp%d" % h, tag="tp")
                 nc.tensor.matmul(bp[:], lhsT=ones[:], rhs=bias_row[:, h * NH : (h + 1) * NH], start=True, stop=True)
                 nc.scalar.copy(out=bias_sb[:, h * NH : (h + 1) * NH], in_=bp[:])
 
-        lo, hi = (0, 1), (2, 3)
-        dummies(6)
-        sort(0)
-        transposes(0, fill=(1, 3))
+        def each(fn, c):
+            for name in CHUNK[c]:
+                fn(name)
+
+        each(sort, 0)
+        each(transposes, 0)
+        each(quant, 0)
+        run_chunk(0, (0, 1))
+        each(sort, 1)
+        each(transposes, 1)
+        run_chunk(0, (2, 3))
+        each(sort, 2)
+        each(quant, 1)
+        each(transposes, 2)
+        run_chunk(1)
+        each(sort, 3)
+        each(quant, 2)
+        each(transposes, 3)
+        run_chunk(2)
+        each(quant, 3)
         bias_spread()
-        quant(0)
-        run_chunk(0, 0, lo)
-        for c in (1, 2, 3):
-            sort(c)
-            transposes(c)
-            run_chunk(0, c - 1, hi)
-            quant(c)
-            run_chunk(0, c, lo)
-        run_chunk(0, 3, hi)
-        sort(4)
-        run_tile(0, 0)
-        run_tile(0, 1)
-        transposes(4)
-        sort(5)
-        quant(4)
-        run_tile(0, 2)
-        transposes(5)
-        sort(6)
-        quant(5)
-        run_tile(0, 3)
-        transposes(6)
-        sort(7)
-        quant(6)
-        run_chunk(1, 0)
-        transposes(7)
-        quant(7)
-        run_chunk(1, 1)
-        run_chunk(1, 2)
-        run_chunk(1, 3)
-        for t in range(QT):
-            run_tile(1, t)
+        run_chunk(3)
+        sort("T4")
+        run_bank(0, 1, 0)
+        sort("T5")
+        run_bank(1, 1, 1)
+        transposes("T4")
+        quant("T4")
+        run_bank(2, 1, 2)
+        v_sort(6, 0)
+        transposes("T5")
+        v_transpose(6, 0)
+        quant("T5")
+        run_bank(3, 1, 3)
+        v_sort(6, 1)
+        v_transpose(6, 1)
+        run_bank(4, 0, 0)
+        v_group(6)
+        v_quant(6)
+        run_bank(4, 1, 1)
+        v_sort(7, 0)
+        v_transpose(7, 0)
+        v_sort(7, 1)
+        run_bank(5, 0, 2)
+        v_transpose(7, 1)
+        v_group(7)
+        run_bank(5, 1, 3)
+        v_quant(7)
+        run_bank(6, 0, 0)
+        run_bank(6, 1, 1)
+        run_bank(7, 0, 2)
+        run_bank(7, 1, 3)

@@ -14,31 +14,22 @@ FP4X4 = mybir.dt.float4_e2m1fn_x4
 P = 128
 M, K, N = 1024, 4096, 1024
 FLOPS = 2 * M * K * N
-NH = 512
-NG = 8
 
-GROUPS = {
-    "c0t0": ((0,), 0, 2),
-    "c0t1": ((1,), 0, 2),
-    "c0t2": ((2,), 0, 2),
-    "c0t3": ((3,), 0, 2),
-    "c1t0": ((0,), 2, 2),
-    "c1t1": ((1,), 2, 2),
-    "c1t2": ((2,), 2, 2),
-    "c1t3": ((3,), 2, 2),
-    "c2t0": ((0, 1), 4, 2),
-    "c2t2": ((2, 3), 4, 2),
-    "c3t0": ((0, 1), 6, 2),
-    "c3t2": ((2, 3), 6, 2),
-    "T4": ((4,), 0, 8),
-    "T5": ((5,), 0, 8),
-}
-CHUNK = {
-    0: ["c0t0", "c0t1", "c0t2", "c0t3"],
-    1: ["c1t0", "c1t1", "c1t2", "c1t3"],
-    2: ["c2t0", "c2t2"],
-    3: ["c3t0", "c3t2"],
-}
+NH = 512
+QT = 4
+CG = 2
+NCH = 4
+
+GROUPS = [
+    [[0], [1], [2], [3]],
+    [[0], [1], [2], [3]],
+    [[0, 1], [2, 3]],
+    [[0, 1], [2, 3]],
+    [[0, 1], [2, 3]],
+    [[0, 1], [2, 3]],
+    [[0, 1], [2, 3]],
+    [[0, 1], [2, 3]],
+]
 
 
 def tile_ant_linear_kernel(tc, x, weight_words, weight_scales, bias, grid, out):
@@ -50,8 +41,8 @@ def tile_ant_linear_kernel(tc, x, weight_words, weight_scales, bias, grid, out):
 
     with ExitStack() as ctx:
         keep = ctx.enter_context(tc.tile_pool(name="keep", bufs=1))
-        rot = ctx.enter_context(tc.tile_pool(name="rot", bufs=2))
-        outp = ctx.enter_context(tc.tile_pool(name="outp", bufs=4))
+        rot = ctx.enter_context(tc.tile_pool(name="rot", bufs=4))
+        outp = ctx.enter_context(tc.tile_pool(name="outp", bufs=6))
         tpp = ctx.enter_context(tc.psum_pool(name="tpp", bufs=4))
         accp = ctx.enter_context(tc.psum_pool(name="accp", bufs=1))
         ctx.enter_context(tc.manual_schedule())
@@ -79,20 +70,19 @@ def tile_ant_linear_kernel(tc, x, weight_words, weight_scales, bias, grid, out):
 
         xt = {}
 
-        def load_x(name):
-            tiles, g0, ng = GROUPS[name]
-            n = len(tiles)
-            t = keep.tile([P, n, ng * 512], BF16, name="x_" + name)
-            r0 = tiles[0] * P
-            nc.sync.dma_start(
-                out=t[:],
-                in_=x2d[r0 : r0 + n * P, g0 * 512 : (g0 + ng) * 512].rearrange("(t p) k -> p t k", p=P),
-            )
-            xt[name] = t
-
-        def load_chunk(c):
-            for name in CHUNK[c]:
-                load_x(name)
+        def load_x(k):
+            q, c = divmod(k, NCH)
+            for gi, grp in enumerate(GROUPS[k]):
+                n = len(grp)
+                t = keep.tile([P, n, CG * 512], BF16, name="x%d_%d" % (k, gi))
+                r0 = (q * QT + grp[0]) * P
+                nc.sync.dma_start(
+                    out=t[:],
+                    in_=x2d[r0 : r0 + n * P, c * CG * 512 : (c + 1) * CG * 512].rearrange(
+                        "(t p) k -> p t k", p=P
+                    ),
+                )
+                xt[(k, gi)] = t
 
         def load_planes(i):
             h, g0, ng = plane_sets[i]
@@ -114,155 +104,125 @@ def tile_ant_linear_kernel(tc, x, weight_words, weight_scales, bias, grid, out):
             for j in range(ng):
                 wmap[(h, g0 + j)] = (t, j)
 
-        xv = {}
-
-        def load_v(t):
-            v = keep.tile([P, 4 * NG, P], BF16, name="xv%d" % t)
-            src = x2d[t * P : (t + 1) * P, :].rearrange("(j mb) (g kb kk) -> kb j mb g kk", mb=4, kb=4, kk=P)
-            for kb in range(4):
-                nc.sync.dma_start(
-                    out=v[32 * kb : 32 * kb + 32].rearrange("p (mb g) kk -> p mb g kk", mb=4), in_=src[kb]
-                )
-            xv[t] = v
-
-        load_chunk(0)
+        load_x(0)
         load_planes(0)
         load_w(0, 0, 2)
-        load_chunk(1)
-        load_chunk(2)
+        load_x(1)
+        load_x(2)
         load_planes(1)
         load_w(0, 2, 2)
-        load_chunk(3)
+        load_x(3)
         load_w(0, 4, 2)
         load_w(0, 6, 2)
         load_planes(2)
         load_w(1, 0, 4)
         load_w(1, 4, 4)
-        load_x("T4")
-        load_x("T5")
-        load_v(6)
-        load_v(7)
+        for k in range(4, 8):
+            load_x(k)
 
         xs = {}
         gr = {}
         cmap = {}
 
-        def sort(name):
-            tiles, g0, ng = GROUPS[name]
-            n = len(tiles)
-            s = rot.tile([P, n, ng, 2, P], F32, name="xs_" + name, tag="xs%d" % (n * ng), bufs=4 if n * ng == 2 else 2)
-            nc.vector.tensor_copy(
-                out=s[:], in_=xt[name][:].bitcast(F32).rearrange("p n (g q u) -> p n g u q", g=ng, u=2)
-            )
-            xs[name] = s
-
-        def transposes(name):
-            tiles, g0, ng = GROUPS[name]
-            n = len(tiles)
-            g_t = rot.tile(
-                [P, n, ng, P, 4], BF16, name="gr_" + name, tag="gr%d" % (n * ng), bufs=4 if n * ng == 2 else 2,
-                align_bytes=64,
-            )
-            gr[name] = g_t
-            for j in range(n):
-                for gp in range(ng // 2):
-                    tp = tpp.tile([P, 2, 2, P], F32, name="tp_%s_%d_%d" % (name, j, gp), tag="tp")
-                    for g2 in range(2):
-                        for u in range(2):
-                            nc.tensor.transpose(tp[:, g2, u, :], xs[name][:, j, 2 * gp + g2, u, :], ident[:])
-                    nc.scalar.copy(
-                        out=g_t[:, j, 2 * gp : 2 * gp + 2].bitcast(F32), in_=tp[:].rearrange("p g u m -> p g m u")
-                    )
-
-        def quantise(name, tiles, g0, ng, grouped):
-            n = len(tiles)
-            cd = keep.tile([P, n * ng * P], U32, name="cd_" + name, align_bytes=64)
-            sc = keep.tile([P, n * ng * P], U8, name="sc_" + name, align_bytes=64)
-            nc.vector.quantize_mx(out=cd[:].bitcast(FP8X4), scales=sc[:], in_=grouped)
-            for j, t in enumerate(tiles):
-                for g in range(ng):
-                    cmap[(t, g0 + g)] = (cd, sc, j * ng + g)
-
-        def quant(name):
-            tiles, g0, ng = GROUPS[name]
-            quantise(name, tiles, g0, ng, gr[name][:].rearrange("p n g m k -> p (n g m k)"))
-
-        s1 = {}
-        o1 = {}
-        grv = {}
-
-        def v_sort(t, a):
-            s = rot.tile([P, 2 * NG, 2, 32], F32, name="s1_%d_%d" % (t, a), tag="s1", align_bytes=64)
-            nc.scalar.copy(
-                out=s[:],
-                in_=xv[t][:, 2 * NG * a : 2 * NG * (a + 1)].bitcast(F32).rearrange("p b (i u) -> p b u i", u=2),
-            )
-            s1[(t, a)] = s
-
-        def v_transpose(t, a):
-            o = rot.tile([P, 2 * NG, 2, 32], F32, name="o1_%d_%d" % (t, a), tag="o1", align_bytes=64)
-            nc.vector.transpose(
-                out=o[:].rearrange("p b u j -> p (b u j)"), in_=s1[(t, a)][:].rearrange("p b u i -> p (b u i)")
-            )
-            o1[(t, a)] = o
-
-        def v_group(t):
-            g_t = rot.tile([P, 1, NG, P, 4], BF16, name="grv%d" % t, tag="gr8", align_bytes=64)
-            grv[t] = g_t
-            gf = g_t[:, 0].bitcast(F32)
-            for mb in range(4):
-                a, m2 = divmod(mb, 2)
-                nc.scalar.copy(
-                    out=gf[:, :, 32 * mb : 32 * mb + 32, :],
-                    in_=o1[(t, a)][:, NG * m2 : NG * (m2 + 1)].rearrange("p g u j -> p g j u"),
+        def sort(k):
+            for gi, grp in enumerate(GROUPS[k]):
+                n = len(grp)
+                s = rot.tile([P, n, CG, 2, P], F32, name="xs%d_%d" % (k, gi), tag="xs%d" % n)
+                nc.vector.tensor_copy(
+                    out=s[:],
+                    in_=xt[(k, gi)][:].bitcast(F32).rearrange("p n (g q u) -> p n g u q", g=CG, u=2),
                 )
+                xs[(k, gi)] = s
 
-        def v_quant(t):
-            quantise("v%d" % t, (t,), 0, NG, grv[t][:].rearrange("p n g m k -> p (n g m k)"))
+        def transposes(k):
+            for gi, grp in enumerate(GROUPS[k]):
+                n = len(grp)
+                g_t = rot.tile([P, n, CG, P, 4], BF16, name="gr%d_%d" % (k, gi), tag="gr%d" % n, align_bytes=64)
+                gr[(k, gi)] = g_t
+                for j in range(n):
+                    tp = tpp.tile([P, CG, 2, P], F32, name="tp%d_%d_%d" % (k, gi, j), tag="tp")
+                    for g2 in range(CG):
+                        for u in range(2):
+                            nc.tensor.transpose(tp[:, g2, u, :], xs[(k, gi)][:, j, g2, u, :], ident[:])
+                    nc.scalar.copy(out=g_t[:, j].bitcast(F32), in_=tp[:].rearrange("p g u m -> p g m u"))
+
+        def quant(k):
+            q, c = divmod(k, NCH)
+            for gi, grp in enumerate(GROUPS[k]):
+                n = len(grp)
+                cd = keep.tile([P, n * CG * P], U32, name="cd%d_%d" % (k, gi), align_bytes=64)
+                sc = keep.tile([P, n * CG * P], U8, name="sc%d_%d" % (k, gi), align_bytes=64)
+                nc.vector.quantize_mx(
+                    out=cd[:].bitcast(FP8X4),
+                    scales=sc[:],
+                    in_=gr[(k, gi)][:].rearrange("p n g m k -> p (n g m k)"),
+                )
+                for j, t in enumerate(grp):
+                    for g2 in range(CG):
+                        cmap[(q, t, c * CG + g2)] = (cd, sc, j * CG + g2)
 
         acc = {}
 
-        def mx(t, g, h, bank):
-            cd, sc, i = cmap[(t, g)]
+        def mx(q, t, g, h):
+            cd, sc, i = cmap[(q, t, g)]
             w, wj = wmap[(h, g)]
             wp, pj = pmap[(h, g)]
             if g == 0:
-                acc[bank] = accp.tile([P, NH], F32, name="acc%d_%d" % (t, h), tag="acc%d" % bank)
+                acc[t] = accp.tile([P, NH], F32, name="acc%d_%d_%d" % (q, h, t), tag="acc%d" % t)
             nc.tensor.matmul_mx(
-                out=acc[bank][:],
+                out=acc[t][:],
                 lhsT=cd[:, i * P : (i + 1) * P].bitcast(FP8X4),
                 lhsT_scale=sc[:, i * P : (i + 1) * P],
                 rhs=w[:, wj, :].bitcast(FP4X4),
                 rhs_scale=wp[:, pj, :],
                 start=(g == 0),
-                stop=(g == NG - 1),
+                stop=(g == 7),
             )
 
-        def finish(t, h, bank):
-            o = outp.tile([P, NH], F32, name="o%d_%d" % (t, h), tag="o")
+        def finish(q, t, h):
+            o = outp.tile([P, NH], F32, name="o%d_%d_%d" % (q, h, t), tag="o")
             nc.vector.tensor_tensor(
-                out=o[:], in0=acc[bank][:], in1=bias_sb[:, h * NH : (h + 1) * NH], op=mybir.AluOpType.add
+                out=o[:], in0=acc[t][:], in1=bias_sb[:, h * NH : (h + 1) * NH], op=mybir.AluOpType.add
             )
-            r0 = t * P
-            if t in xv:
-                for mb in range(4):
-                    nc.sync.dma_start(
-                        out=out2d[r0 + mb : r0 + P : 4, h * NH : (h + 1) * NH], in_=o[32 * mb : 32 * mb + 32, :]
-                    )
-            else:
-                nc.sync.dma_start(out=out2d[r0 : r0 + P, h * NH : (h + 1) * NH], in_=o[:])
+            r0 = (q * QT + t) * P
+            nc.sync.dma_start(out=out2d[r0 : r0 + P, h * NH : (h + 1) * NH], in_=o[:])
 
-        def run_chunk(c, tiles=(0, 1, 2, 3)):
+        def run_chunk(q, c, tiles=(0, 1, 2, 3)):
             for t in tiles:
-                for g2 in range(2):
-                    mx(t, 2 * c + g2, 0, t)
-                if c == 3:
-                    finish(t, 0, t)
+                for g2 in range(CG):
+                    mx(q, t, c * CG + g2, 0)
+                if c == NCH - 1:
+                    finish(q, t, 0)
 
-        def run_bank(t, h, bank):
-            for g in range(NG):
-                mx(t, g, h, bank)
-            finish(t, h, bank)
+        def run_tile(q, t):
+            for g in range(8):
+                mx(q, t, g, 1)
+            finish(q, t, 1)
+
+        def run_last(q, t):
+            NQ = 128
+            r0 = (q * QT + t) * P
+            for nq in range(4):
+                a = accp.tile([P, NH], F32, name="accl%d" % nq, tag="acc%d" % ((t + nq) % 4))
+                for g in range(8):
+                    cd, sc, i = cmap[(q, t, g)]
+                    w, wj = wmap[(1, g)]
+                    wp, pj = pmap[(1, g)]
+                    nc.tensor.matmul_mx(
+                        out=a[:, 0:NQ],
+                        lhsT=cd[:, i * P : (i + 1) * P].bitcast(FP8X4),
+                        lhsT_scale=sc[:, i * P : (i + 1) * P],
+                        rhs=w[:, wj, 2 * NQ * nq : 2 * NQ * (nq + 1)].bitcast(FP4X4),
+                        rhs_scale=wp[:, pj, NQ * nq : NQ * (nq + 1)],
+                        start=(g == 0),
+                        stop=(g == 7),
+                    )
+                o = outp.tile([P, NH], F32, name="ol%d" % nq, tag="o")
+                c0 = NH + NQ * nq
+                nc.vector.tensor_tensor(
+                    out=o[:, 0:NQ], in0=a[:, 0:NQ], in1=bias_sb[:, c0 : c0 + NQ], op=mybir.AluOpType.add
+                )
+                nc.sync.dma_start(out=out2d[r0 : r0 + P, c0 : c0 + NQ], in_=o[:, 0:NQ])
 
         def bias_spread():
             for h in range(2):
@@ -270,55 +230,44 @@ def tile_ant_linear_kernel(tc, x, weight_words, weight_scales, bias, grid, out):
                 nc.tensor.matmul(bp[:], lhsT=ones[:], rhs=bias_row[:, h * NH : (h + 1) * NH], start=True, stop=True)
                 nc.scalar.copy(out=bias_sb[:, h * NH : (h + 1) * NH], in_=bp[:])
 
-        def each(fn, c):
-            for name in CHUNK[c]:
-                fn(name)
-
-        each(sort, 0)
-        each(transposes, 0)
-        each(quant, 0)
-        run_chunk(0, (0, 1))
-        each(sort, 1)
-        each(transposes, 1)
-        run_chunk(0, (2, 3))
-        each(sort, 2)
-        each(quant, 1)
-        each(transposes, 2)
-        run_chunk(1)
-        each(sort, 3)
-        each(quant, 2)
-        each(transposes, 3)
-        run_chunk(2)
-        each(quant, 3)
+        sort(0)
+        transposes(0)
+        quant(0)
+        run_chunk(0, 0, (0, 1))
+        sort(1)
+        transposes(1)
+        run_chunk(0, 0, (2, 3))
+        sort(2)
+        quant(1)
+        transposes(2)
+        run_chunk(0, 1)
+        sort(3)
+        quant(2)
+        transposes(3)
+        run_chunk(0, 2)
+        quant(3)
         bias_spread()
-        run_chunk(3)
-        sort("T4")
-        run_bank(0, 1, 0)
-        sort("T5")
-        run_bank(1, 1, 1)
-        transposes("T4")
-        quant("T4")
-        run_bank(2, 1, 2)
-        v_sort(6, 0)
-        transposes("T5")
-        v_transpose(6, 0)
-        quant("T5")
-        run_bank(3, 1, 3)
-        v_sort(6, 1)
-        v_transpose(6, 1)
-        run_bank(4, 0, 0)
-        v_group(6)
-        v_quant(6)
-        run_bank(4, 1, 1)
-        v_sort(7, 0)
-        v_transpose(7, 0)
-        v_sort(7, 1)
-        run_bank(5, 0, 2)
-        v_transpose(7, 1)
-        v_group(7)
-        run_bank(5, 1, 3)
-        v_quant(7)
-        run_bank(6, 0, 0)
-        run_bank(6, 1, 1)
-        run_bank(7, 0, 2)
-        run_bank(7, 1, 3)
+        run_chunk(0, 3)
+        sort(4)
+        run_tile(0, 0)
+        run_tile(0, 1)
+        transposes(4)
+        sort(5)
+        quant(4)
+        run_tile(0, 2)
+        transposes(5)
+        sort(6)
+        quant(5)
+        run_tile(0, 3)
+        transposes(6)
+        sort(7)
+        quant(6)
+        run_chunk(1, 0)
+        transposes(7)
+        quant(7)
+        run_chunk(1, 1)
+        run_chunk(1, 2)
+        run_chunk(1, 3)
+        for t in range(QT - 1):
+            run_tile(1, t)
+        run_last(1, QT - 1)

from contextlib import ExitStack

import concourse.mybir as mybir
from concourse.masks import make_identity

BF16 = mybir.dt.bfloat16
F32 = mybir.dt.float32
I32 = mybir.dt.int32
U8 = mybir.dt.uint8
U32 = mybir.dt.uint32
FP8X4 = mybir.dt.float8_e4m3fn_x4
FP4X4 = mybir.dt.float4_e2m1fn_x4

P = 128
M, K, N = 1024, 4096, 1024
FLOPS = 2 * M * K * N

NH = 512
QT = 4
CG = 2
NCH = 4

GROUPS = [
    [[0], [1], [2], [3]],
    [[0], [1], [2], [3]],
    [[0, 1], [2, 3]],
    [[0, 1], [2, 3]],
    [[0, 1], [2, 3]],
    [[0, 1], [2, 3]],
    [[0, 1], [2, 3]],
    [[0, 1], [2, 3]],
]


def tile_ant_linear_kernel(tc, x, weight_words, weight_scales, bias, grid, out):
    nc = tc.nc
    x2d = x.flatten_outer_dims()
    out2d = out.flatten_outer_dims()
    ww = weight_words.bitcast(I32)
    ws = weight_scales.bitcast(I32)

    with ExitStack() as ctx:
        keep = ctx.enter_context(tc.tile_pool(name="keep", bufs=1))
        rot = ctx.enter_context(tc.tile_pool(name="rot", bufs=4))
        outp = ctx.enter_context(tc.tile_pool(name="outp", bufs=6))
        tpp = ctx.enter_context(tc.psum_pool(name="tpp", bufs=4))
        accp = ctx.enter_context(tc.psum_pool(name="accp", bufs=1))
        ctx.enter_context(tc.manual_schedule())

        plane_sets = [(0, 0, 2), (0, 2, 6), (1, 0, 8)]
        planes = []
        pmap = {}
        for i, (h, g0, ng) in enumerate(plane_sets):
            wp = keep.tile([P, ng, NH], U8, name="wp%d" % i, align_bytes=64)
            planes.append(wp)
            for j in range(ng):
                pmap[(h, g0 + j)] = (wp, j)
        bias_row = keep.tile([P, N], BF16, name="bias_row")
        bias_sb = keep.tile([P, N], F32, name="bias_sb")
        ones = keep.tile([P, P], BF16, name="ones")
        ident = keep.tile([P, P], F32, name="ident")

        nc.vector.memset(planes[0][:].bitcast(I32), 0)
        nc.vector.memset(bias_row[:].bitcast(I32), 0)
        nc.vector.memset(planes[1][:].bitcast(I32), 0)
        nc.vector.memset(planes[2][:].bitcast(I32), 0)
        make_identity(nc, ident[:])
        nc.gpsimd.memset(ones[:], 1.0)
        nc.scalar.dma_start(out=bias_row[0:1, :], in_=bias.rearrange("(o n) -> o n", o=1))

        xt = {}

        def load_x(k):
            q, c = divmod(k, NCH)
            for gi, grp in enumerate(GROUPS[k]):
                n = len(grp)
                t = keep.tile([P, n, CG * 512], BF16, name="x%d_%d" % (k, gi))
                r0 = (q * QT + grp[0]) * P
                nc.sync.dma_start(
                    out=t[:],
                    in_=x2d[r0 : r0 + n * P, c * CG * 512 : (c + 1) * CG * 512].rearrange(
                        "(t p) k -> p t k", p=P
                    ),
                )
                xt[(k, gi)] = t

        def load_planes(i):
            h, g0, ng = plane_sets[i]
            wpi = planes[i][:].bitcast(I32)
            for r in range(4):
                nc.sync.dma_start(
                    out=wpi[r:P:32, :, :],
                    in_=ws[g0 : g0 + ng, r:16:4, h * 128 : (h + 1) * 128].rearrange("g q n -> q g n"),
                )

        wmap = {}

        def load_w(h, g0, ng):
            t = keep.tile([P, ng, 2 * NH], U8, name="w%d_%d" % (h, g0), align_bytes=64)
            nc.sync.dma_start(
                out=t[:].bitcast(I32),
                in_=ww[g0 : g0 + ng, :, h * 256 : (h + 1) * 256].rearrange("g p b -> p g b"),
            )
            for j in range(ng):
                wmap[(h, g0 + j)] = (t, j)

        load_x(0)
        load_planes(0)
        load_w(0, 0, 2)
        load_x(1)
        load_x(2)
        load_planes(1)
        load_w(0, 2, 2)
        load_x(3)
        load_w(0, 4, 2)
        load_w(0, 6, 2)
        load_planes(2)
        load_w(1, 0, 4)
        load_w(1, 4, 4)
        for k in range(4, 8):
            load_x(k)

        xs = {}
        gr = {}
        cmap = {}

        def sort(k):
            for gi, grp in enumerate(GROUPS[k]):
                n = len(grp)
                s = rot.tile([P, n, CG, 2, P], F32, name="xs%d_%d" % (k, gi), tag="xs%d" % n)
                nc.vector.tensor_copy(
                    out=s[:],
                    in_=xt[(k, gi)][:].bitcast(F32).rearrange("p n (g q u) -> p n g u q", g=CG, u=2),
                )
                xs[(k, gi)] = s

        def transposes(k):
            for gi, grp in enumerate(GROUPS[k]):
                n = len(grp)
                g_t = rot.tile([P, n, CG, P, 4], BF16, name="gr%d_%d" % (k, gi), tag="gr%d" % n, align_bytes=64)
                gr[(k, gi)] = g_t
                for j in range(n):
                    tp = tpp.tile([P, CG, 2, P], F32, name="tp%d_%d_%d" % (k, gi, j), tag="tp")
                    for g2 in range(CG):
                        for u in range(2):
                            nc.tensor.transpose(tp[:, g2, u, :], xs[(k, gi)][:, j, g2, u, :], ident[:])
                    nc.scalar.copy(out=g_t[:, j].bitcast(F32), in_=tp[:].rearrange("p g u m -> p g m u"))

        def quant(k):
            q, c = divmod(k, NCH)
            for gi, grp in enumerate(GROUPS[k]):
                n = len(grp)
                cd = keep.tile([P, n * CG * P], U32, name="cd%d_%d" % (k, gi), align_bytes=64)
                sc = keep.tile([P, n * CG * P], U8, name="sc%d_%d" % (k, gi), align_bytes=64)
                nc.vector.quantize_mx(
                    out=cd[:].bitcast(FP8X4),
                    scales=sc[:],
                    in_=gr[(k, gi)][:].rearrange("p n g m k -> p (n g m k)"),
                )
                for j, t in enumerate(grp):
                    for g2 in range(CG):
                        cmap[(q, t, c * CG + g2)] = (cd, sc, j * CG + g2)

        acc = {}

        def mx(q, t, g, h):
            cd, sc, i = cmap[(q, t, g)]
            w, wj = wmap[(h, g)]
            wp, pj = pmap[(h, g)]
            if g == 0:
                acc[t] = accp.tile([P, NH], F32, name="acc%d_%d_%d" % (q, h, t), tag="acc%d" % t)
            nc.tensor.matmul_mx(
                out=acc[t][:],
                lhsT=cd[:, i * P : (i + 1) * P].bitcast(FP8X4),
                lhsT_scale=sc[:, i * P : (i + 1) * P],
                rhs=w[:, wj, :].bitcast(FP4X4),
                rhs_scale=wp[:, pj, :],
                start=(g == 0),
                stop=(g == 7),
            )

        def finish(q, t, h):
            o = outp.tile([P, NH], F32, name="o%d_%d_%d" % (q, h, t), tag="o")
            nc.vector.tensor_tensor(
                out=o[:], in0=acc[t][:], in1=bias_sb[:, h * NH : (h + 1) * NH], op=mybir.AluOpType.add
            )
            r0 = (q * QT + t) * P
            nc.sync.dma_start(out=out2d[r0 : r0 + P, h * NH : (h + 1) * NH], in_=o[:])

        def run_chunk(q, c, tiles=(0, 1, 2, 3)):
            for t in tiles:
                for g2 in range(CG):
                    mx(q, t, c * CG + g2, 0)
                if c == NCH - 1:
                    finish(q, t, 0)

        def run_tile(q, t):
            for g in range(8):
                mx(q, t, g, 1)
            finish(q, t, 1)

        def run_last(q, t):
            NQ = 128
            r0 = (q * QT + t) * P
            for nq in range(4):
                a = accp.tile([P, NH], F32, name="accl%d" % nq, tag="acc%d" % ((t + nq) % 4))
                for g in range(8):
                    cd, sc, i = cmap[(q, t, g)]
                    w, wj = wmap[(1, g)]
                    wp, pj = pmap[(1, g)]
                    nc.tensor.matmul_mx(
                        out=a[:, 0:NQ],
                        lhsT=cd[:, i * P : (i + 1) * P].bitcast(FP8X4),
                        lhsT_scale=sc[:, i * P : (i + 1) * P],
                        rhs=w[:, wj, 2 * NQ * nq : 2 * NQ * (nq + 1)].bitcast(FP4X4),
                        rhs_scale=wp[:, pj, NQ * nq : NQ * (nq + 1)],
                        start=(g == 0),
                        stop=(g == 7),
                    )
                o = outp.tile([P, NH], F32, name="ol%d" % nq, tag="o")
                c0 = NH + NQ * nq
                nc.vector.tensor_tensor(
                    out=o[:, 0:NQ], in0=a[:, 0:NQ], in1=bias_sb[:, c0 : c0 + NQ], op=mybir.AluOpType.add
                )
                nc.sync.dma_start(out=out2d[r0 : r0 + P, c0 : c0 + NQ], in_=o[:, 0:NQ])

        def bias_spread():
            for h in range(2):
                bp = tpp.tile([P, NH], F32, name="bp%d" % h, tag="tp")
                nc.tensor.matmul(bp[:], lhsT=ones[:], rhs=bias_row[:, h * NH : (h + 1) * NH], start=True, stop=True)
                nc.scalar.copy(out=bias_sb[:, h * NH : (h + 1) * NH], in_=bp[:])

        sort(0)
        transposes(0)
        quant(0)
        run_chunk(0, 0, (0, 1))
        sort(1)
        transposes(1)
        run_chunk(0, 0, (2, 3))
        sort(2)
        quant(1)
        transposes(2)
        run_chunk(0, 1)
        sort(3)
        quant(2)
        transposes(3)
        run_chunk(0, 2)
        quant(3)
        bias_spread()
        run_chunk(0, 3)
        sort(4)
        run_tile(0, 0)
        run_tile(0, 1)
        transposes(4)
        sort(5)
        quant(4)
        run_tile(0, 2)
        transposes(5)
        sort(6)
        quant(5)
        run_tile(0, 3)
        transposes(6)
        sort(7)
        quant(6)
        run_chunk(1, 0)
        transposes(7)
        quant(7)
        run_chunk(1, 1)
        run_chunk(1, 2)
        run_chunk(1, 3)
        for t in range(QT - 1):
            run_tile(1, t)
        run_last(1, QT - 1)
